import numpy as np
import ml_dtypes


def mxq(x, axis, fmt="e4m3"):
    dtype, down = {"e4m3": (ml_dtypes.float8_e4m3fn, 7), "e5m2": (ml_dtypes.float8_e5m2, 14)}[fmt]
    v = np.moveaxis(np.asarray(x, np.float32).astype(ml_dtypes.bfloat16).astype(np.float64), axis, -1)
    blocks = v.reshape(v.shape[:-1] + (-1, 32))
    amax = np.abs(blocks).max(-1, keepdims=True)
    byte = np.maximum(np.where(amax > 0, np.frexp(amax)[1] - 1 + 127, 0) - down, 1)
    scale = np.exp2(byte - 127.0)
    codes = (blocks / scale).astype(np.float32).astype(dtype).astype(np.float64)
    return np.moveaxis((codes * scale).reshape(v.shape), -1, axis)


WIDE = False


def mx_kscale(k):
    if not WIDE:
        return np.ones(k)
    levels = np.array([10, -10, 5, -5, 0])
    a = np.random.permutation(np.resize(levels, k // 512 * 4)).reshape(k // 512, 4)
    idx = np.arange(k)
    return np.exp2(a[idx // 512, idx % 128 // 32])


BF16 = ml_dtypes.bfloat16


def bf(x):
    return np.asarray(x, np.float32).astype(BF16)


def f64(x):
    return np.asarray(x).astype(np.float64)


E2M1 = np.array([0.0, 0.5, 1.0, 1.5, 2.0, 3.0, 4.0, 6.0, -0.0, -0.5, -1.0, -1.5, -2.0, -3.0, -4.0, -6.0])


def pack_weight(w, fmt):
    k, n = w.shape
    w = f64(bf(w)).reshape(k // 32, 32, n)
    amax = np.abs(w).max(1)
    if fmt == "e4m3":
        byte = np.frexp(amax)[1] - 1 + 127 - 7
    else:
        mant, ex = np.frexp(amax / 6.0)
        byte = np.where(mant > 0.5, ex, ex - 1) + 127
    byte = np.clip(np.where(amax > 0, byte, 1), 1, 254)
    scaled = (w * np.exp2(127.0 - byte)[:, None, :]).reshape(k, n).astype(np.float32)
    by_word = np.ascontiguousarray(scaled.reshape(k // 512, 128, 4, n).transpose(0, 1, 3, 2))
    if fmt == "e4m3":
        words = by_word.astype(ml_dtypes.float8_e4m3fn).view(np.uint8)
    else:
        c = by_word.astype(ml_dtypes.float4_e2m1fn).view(np.uint8) & 0xF
        words = c[..., 0::2] | (c[..., 1::2] << 4)
    return np.ascontiguousarray(words), np.ascontiguousarray(byte.astype(np.uint8).reshape(k // 512, 16, n))


def unpack_weight(words, scales, fmt):
    g, p, n, _ = words.shape
    if fmt == "e4m3":
        vals = np.ascontiguousarray(words).view(ml_dtypes.float8_e4m3fn).astype(np.float64)
    else:
        nib = np.empty((g, p, n, 4), np.uint8)
        nib[..., 0::2] = words & 0xF
        nib[..., 1::2] = words >> 4
        vals = E2M1[nib]
    vals = vals * np.repeat(np.exp2(scales.astype(np.float64) - 127.0), 8, axis=1)[..., None]
    return vals.transpose(0, 1, 3, 2).reshape(g * 512, n)


B, I, H = 128, 2048, 1024


def sig(v):
    return 1.0 / (1.0 + np.exp(-v))


def setup_inputs():
    s, t = mx_kscale(I), mx_kscale(H)
    x = bf(np.random.standard_normal((B, I)) * s)
    m_prev = bf(np.random.standard_normal((B, H)) * t)
    c_prev = bf(np.random.standard_normal((B, H)))
    w_m_words, w_m_scales = pack_weight(np.random.standard_normal((H, 8 * H)) / np.sqrt(H) / t[:, None], "e4m3")
    w_inputs_words, w_inputs_scales = pack_weight(np.random.standard_normal((I, 8 * H)) / np.sqrt(I) / s[:, None], "e4m3")
    return {"x": x,
            "m_prev": m_prev,
            "c_prev": c_prev,
            "w_m_words": w_m_words,
            "w_m_scales": w_m_scales,
            "w_inputs_words": w_inputs_words,
            "w_inputs_scales": w_inputs_scales}


def reference(x, m_prev, c_prev, w_m_words, w_m_scales, w_inputs_words, w_inputs_scales):
    m_mat = mxq(f64(m_prev), 1, "e4m3") @ unpack_weight(w_m_words, w_m_scales, "e4m3")
    in_mat = mxq(f64(x), 1, "e4m3") @ unpack_weight(w_inputs_words, w_inputs_scales, "e4m3")
    ms = np.split(m_mat, 8, axis=1)
    xs = np.split(in_mat, 8, axis=1)
    l1_0 = sig(xs[0] + ms[0])
    l1_1 = np.maximum(xs[1] + ms[1], 0.0)
    l1_2 = sig(xs[2] + ms[2])
    l1_3 = np.maximum(xs[3] * ms[3], 0.0)
    l1_4 = np.tanh(xs[4] + ms[4])
    l1_5 = sig(xs[5] + ms[5])
    l1_6 = np.tanh(xs[6] + ms[6])
    l1_7 = sig(xs[7] + ms[7])
    l2_0 = np.tanh(l1_0 * l1_1)
    l2_1 = np.tanh(l1_2 + l1_3)
    l2_2 = np.tanh(l1_4 * l1_5)
    l2_3 = sig(l1_6 + l1_7)
    l2_0 = np.tanh(l2_0 + f64(c_prev))
    new_c = l2_0 * l2_1
    l3_1 = np.tanh(l2_2 + l2_3)
    new_m = np.tanh(new_c * l3_1)
    return (new_m, new_c)

@@ -1,0 +1,209 @@
+from contextlib import ExitStack
+
+import concourse.masks as masks
+import concourse.mybir as mybir
+
+F32 = mybir.dt.float32
+BF16 = mybir.dt.bfloat16
+I32 = mybir.dt.int32
+U32 = mybir.dt.uint32
+U8 = mybir.dt.uint8
+FP8X4 = mybir.dt.float8_e4m3fn_x4
+ACT = mybir.ActivationFunctionType
+ALU = mybir.AluOpType
+
+P = 128
+H = 1024
+G_M = 2
+G_X = 4
+G_ALL = G_M + G_X
+BANK = 512
+W_SLOT = 4096
+W_BUFS = 10
+
+FLOPS = 2 * 128 * (1024 + 2048) * 8192
+
+
+def tile_nascell_w_kernel(
+    tc, x, m_prev, c_prev, w_m_words, w_m_scales, w_inputs_words, w_inputs_scales, out_0, out_1
+):
+    nc = tc.nc
+    wm_words = w_m_words.rearrange("g p n t -> g p (n t)").bitcast(I32)
+    wi_words = w_inputs_words.rearrange("g p n t -> g p (n t)").bitcast(I32)
+    wm_scales = w_m_scales.bitcast(I32)
+    wi_scales = w_inputs_scales.bitcast(I32)
+
+    with ExitStack() as ctx:
+        const = ctx.enter_context(tc.tile_pool(name="const", bufs=1))
+        wpool = ctx.enter_context(tc.tile_pool(name="wring", bufs=W_BUFS))
+        psum = ctx.enter_context(tc.psum_pool(name="psum", bufs=8))
+        ctx.enter_context(tc.manual_schedule())
+
+        m_sb = const.tile([P, H], BF16, name="m_sb")
+        x_sb = const.tile([P, 2 * H], BF16, name="x_sb")
+        c_sb = const.tile([P, H], BF16, name="c_sb")
+        nc.sync.dma_start(out=m_sb[:], in_=m_prev)
+        nc.sync.dma_start(out=x_sb[:], in_=x)
+
+        planes_m = const.tile([P, G_M * 2048], U8, name="planes_m", align_bytes=64)
+        planes_x = const.tile([P, 8 * H], U8, name="planes_x", align_bytes=64)
+        nc.vector.memset(planes_m[:].bitcast(I32), 0)
+        nc.vector.memset(planes_x[:].bitcast(I32), 0)
+
+        warm = const.tile([P, 16], F32, name="warm")
+        nc.vector.memset(warm[:], 0.0)
+        nc.scalar.activation(out=warm[:, 8:16], in_=warm[:, 0:8], func=ACT.Sigmoid)
+
+        ident = const.tile([P, P], F32, name="ident")
+        masks.make_identity(nc, ident[:])
+
+        for g in range(G_M):
+            for q in range(4):
+                nc.sync.dma_start(
+                    out=planes_m[32 * q : 32 * q + 16, 2048 * g : 2048 * (g + 1)].bitcast(I32),
+                    in_=wm_scales[g, 4 * q : 4 * q + 4, :].rearrange("r (j n) -> j r n", j=4),
+                )
+        for q in range(4):
+            nc.sync.dma_start(
+                out=planes_x[32 * q : 32 * q + 16, :].bitcast(I32),
+                in_=wi_scales[:, 4 * q : 4 * q + 4, :],
+            )
+
+        grouped = const.tile([P, G_ALL * 512], BF16, name="grouped", align_bytes=64)
+        grouped_w = grouped[:].bitcast(F32).rearrange("p (s b u) -> p s b u", s=G_ALL, u=2)
+        codes = const.tile([P, G_ALL * P], U32, name="codes", align_bytes=64)
+        a_scales = const.tile([P, G_ALL * P], U8, name="a_scales", align_bytes=64)
+
+        def transpose_two_groups(src_words, g0, s0, copy):
+            tp = psum.tile([P, 2, 2, P], F32, tag="bank", name="tp%d" % s0)
+            for g in range(2):
+                for u in range(2):
+                    lo = 256 * (g0 + g) + u
+                    nc.tensor.transpose(tp[:, g, u, :], src_words[:, lo : lo + 255 : 2], ident[:])
+            copy(out=grouped_w[:, s0 : s0 + 2], in_=tp[:].rearrange("p g u b -> p g b u"))
+
+        m_words = m_sb[:].bitcast(F32)
+        x_words = x_sb[:].bitcast(F32)
+        transpose_two_groups(m_words, 0, 0, nc.vector.tensor_copy)
+        transpose_two_groups(x_words, 0, 2, nc.scalar.copy)
+        transpose_two_groups(x_words, 2, 4, nc.vector.tensor_copy)
+        nc.vector.quantize_mx(
+            out=codes[:, 0 : G_M * P].bitcast(FP8X4),
+            scales=a_scales[:, 0 : G_M * P],
+            in_=grouped[:, 0 : G_M * 512],
+        )
+        nc.vector.quantize_mx(
+            out=codes[:, G_M * P :].bitcast(FP8X4),
+            scales=a_scales[:, G_M * P :],
+            in_=grouped[:, G_M * 512 :],
+        )
+
+        def load_w(s, n0, n):
+            wt = wpool.tile([P, W_SLOT], U32, tag="w", name="w%d_%d" % (s, n0), align_bytes=64)
+            src = wm_words[s] if s < G_M else wi_words[s - G_M]
+            nc.sync.dma_start(out=wt[:, 0:n].bitcast(I32), in_=src[:, n0 : n0 + n])
+            return wt
+
+        def plane(s, n0, n):
+            if s < G_M:
+                k = 4 * (n0 // 2048)
+                lo = 2048 * s + n0 % 2048
+                return planes_m[k:P, lo : lo + n]
+            return planes_x[4 * (s - G_M) : P, n0 : n0 + n]
+
+        def mx_pass(acc, s, wt, off, n0, n, first, last):
+            nc.tensor.matmul_mx(
+                out=acc,
+                lhsT=codes[:, P * s : P * (s + 1)].bitcast(FP8X4),
+                lhsT_scale=a_scales[:, P * s : P * (s + 1)],
+                rhs=wt[:, off : off + n].bitcast(FP8X4),
+                rhs_scale=plane(s, n0, n),
+                start=(s == first),
+                stop=(s == last),
+            )
+
+        def bank(name):
+            return psum.tile([P, BANK], F32, tag="bank", name=name)
+
+        va = const.tile([P, H], F32, name="va")
+        vb = const.tile([P, H], F32, name="vb")
+        vc = const.tile([P, H], F32, name="vc")
+        vd = const.tile([P, H], F32, name="vd")
+        ve = const.tile([P, H], F32, name="ve")
+        vf = const.tile([P, H], F32, name="vf")
+        vg = const.tile([P, H], F32, name="vg")
+
+        acc = [bank("p47_%d" % c) for c in range(8)]
+        for s in range(G_ALL):
+            wt = load_w(s, 4 * H, 4 * H)
+            for c in range(8):
+                mx_pass(acc[c][:], s, wt, BANK * c, 4 * H + BANK * c, BANK, 0, G_ALL - 1)
+        for h in range(2):
+            cols = slice(BANK * h, BANK * (h + 1))
+            nc.scalar.activation(out=va[:, cols], in_=acc[0 + h][:], func=ACT.Tanh)
+            nc.scalar.activation(out=vb[:, cols], in_=acc[2 + h][:], func=ACT.Sigmoid)
+            nc.scalar.activation(out=vc[:, cols], in_=acc[4 + h][:], func=ACT.Tanh)
+            nc.scalar.activation(out=vd[:, cols], in_=acc[6 + h][:], func=ACT.Sigmoid)
+        for h in range(2):
+            cols = slice(BANK * h, BANK * (h + 1))
+            nc.vector.tensor_tensor(out=va[:, cols], in0=va[:, cols], in1=vb[:, cols], op=ALU.mult)
+            nc.vector.tensor_tensor(out=vc[:, cols], in0=vc[:, cols], in1=vd[:, cols], op=ALU.add)
+            nc.scalar.activation(out=va[:, cols], in_=va[:, cols], func=ACT.Tanh)
+            nc.scalar.activation(out=vc[:, cols], in_=vc[:, cols], func=ACT.Sigmoid)
+            nc.vector.tensor_tensor(out=va[:, cols], in0=va[:, cols], in1=vc[:, cols], op=ALU.add)
+            nc.scalar.activation(out=va[:, cols], in_=va[:, cols], func=ACT.Tanh)
+
+        nc.sync.dma_start(out=c_sb[:], in_=c_prev)
+        acc = [bank("p01_%d" % c) for c in range(4)]
+        for s in range(G_ALL):
+            wt = load_w(s, 0, 2 * H)
+            for c in range(4):
+                mx_pass(acc[c][:], s, wt, BANK * c, BANK * c, BANK, 0, G_ALL - 1)
+        for h in range(2):
+            cols = slice(BANK * h, BANK * (h + 1))
+            nc.scalar.activation(out=ve[:, cols], in_=acc[h][:], func=ACT.Sigmoid)
+            nc.vector.scalar_tensor_tensor(
+                out=ve[:, cols], in0=acc[2 + h][:], scalar=0.0, in1=ve[:, cols], op0=ALU.max, op1=ALU.mult
+            )
+            nc.scalar.activation(out=ve[:, cols], in_=ve[:, cols], func=ACT.Tanh)
+            nc.vector.tensor_tensor(out=ve[:, cols], in0=ve[:, cols], in1=c_sb[:, cols], op=ALU.add)
+            nc.scalar.activation(out=ve[:, cols], in_=ve[:, cols], func=ACT.Tanh)
+            nc.vector.tensor_tensor(out=va[:, cols], in0=va[:, cols], in1=ve[:, cols], op=ALU.mult)
+
+        chunks = [(0, 512), (512, 256), (768, 256)]
+        acc2 = [bank("p2_%d" % h) for h in range(2)]
+        accm = [bank("pm3_%d" % h) for h in range(2)]
+        for s in range(G_M):
+            wt = load_w(s, 2 * H, 2 * H)
+            for h in range(2):
+                mx_pass(acc2[h][:], s, wt, BANK * h, 2 * H + BANK * h, BANK, 0, G_ALL - 1)
+            for h in range(2):
+                mx_pass(accm[h][:], s, wt, H + BANK * h, 3 * H + BANK * h, BANK, 0, G_M - 1)
+        for h in range(2):
+            nc.vector.tensor_copy(out=vf[:, BANK * h : BANK * (h + 1)], in_=accm[h][:])
+        accx = [bank("px3_%d" % i) for i in range(len(chunks))]
+        for s in range(G_M, G_ALL - 1):
+            wt = load_w(s, 2 * H, 2 * H)
+            for h in range(2):
+                mx_pass(acc2[h][:], s, wt, BANK * h, 2 * H + BANK * h, BANK, 0, G_ALL - 1)
+            for i, (c0, n) in enumerate(chunks):
+                mx_pass(accx[i][:, 0:n], s, wt, H + c0, 3 * H + c0, n, G_M, G_ALL - 1)
+        s = G_ALL - 1
+        wt = load_w(s, 2 * H, H)
+        for h in range(2):
+            mx_pass(acc2[h][:], s, wt, BANK * h, 2 * H + BANK * h, BANK, 0, G_ALL - 1)
+            nc.scalar.activation(out=vg[:, BANK * h : BANK * (h + 1)], in_=acc2[h][:], func=ACT.Sigmoid)
+        for i, (c0, n) in enumerate(chunks):
+            cols = slice(c0, c0 + n)
+            wt = load_w(s, 3 * H + c0, n)
+            mx_pass(accx[i][:, 0:n], s, wt, 0, 3 * H + c0, n, G_M, G_ALL - 1)
+            nc.vector.tensor_tensor(out=vf[:, cols], in0=accx[i][:, 0:n], in1=vf[:, cols], op=ALU.mult)
+            nc.vector.scalar_tensor_tensor(
+                out=vg[:, cols], in0=vf[:, cols], scalar=0.0, in1=vg[:, cols], op0=ALU.max, op1=ALU.add
+            )
+            nc.scalar.activation(out=vg[:, cols], in_=vg[:, cols], func=ACT.Tanh)
+            nc.vector.tensor_tensor(out=va[:, cols], in0=va[:, cols], in1=vg[:, cols], op=ALU.mult)
+            nc.vector.tensor_tensor(out=ve[:, cols], in0=ve[:, cols], in1=vg[:, cols], op=ALU.mult)
+            nc.scalar.activation(out=va[:, cols], in_=va[:, cols], func=ACT.Tanh)
+            nc.sync.dma_start(out=out_1[:, cols], in_=ve[:, cols])
+            nc.sync.dma_start(out=out_0[:, cols], in_=va[:, cols])

@@ -18,8 +18,9 @@ G_M = 2
 G_X = 4
 G_ALL = G_M + G_X
 BANK = 512
-W_SLOT = 4096
-W_BUFS = 10
+CH = 256
+N_CH = H // CH
+Z_FIRST = 3
 
 FLOPS = 2 * 128 * (1024 + 2048) * 8192
 
@@ -35,7 +36,7 @@ def tile_nascell_w_kernel(
 
     with ExitStack() as ctx:
         const = ctx.enter_context(tc.tile_pool(name="const", bufs=1))
-        wpool = ctx.enter_context(tc.tile_pool(name="wring", bufs=W_BUFS))
+        wpool = ctx.enter_context(tc.tile_pool(name="wring", bufs=6))
         psum = ctx.enter_context(tc.psum_pool(name="psum", bufs=8))
         ctx.enter_context(tc.manual_schedule())
 
@@ -98,10 +99,10 @@ def tile_nascell_w_kernel(
             in_=grouped[:, G_M * 512 :],
         )
 
-        def load_w(s, n0, n):
-            wt = wpool.tile([P, W_SLOT], U32, tag="w", name="w%d_%d" % (s, n0), align_bytes=64)
+        def load_w(s, n0, n, tag, bufs):
+            wt = wpool.tile([P, n], U32, tag=tag, bufs=bufs, name="w%d_%d" % (s, n0), align_bytes=64)
             src = wm_words[s] if s < G_M else wi_words[s - G_M]
-            nc.sync.dma_start(out=wt[:, 0:n].bitcast(I32), in_=src[:, n0 : n0 + n])
+            nc.sync.dma_start(out=wt[:].bitcast(I32), in_=src[:, n0 : n0 + n])
             return wt
 
         def plane(s, n0, n):
@@ -125,6 +126,9 @@ def tile_nascell_w_kernel(
         def bank(name):
             return psum.tile([P, BANK], F32, tag="bank", name=name)
 
+        def half(h):
+            return slice(BANK * h, BANK * (h + 1))
+
         va = const.tile([P, H], F32, name="va")
         vb = const.tile([P, H], F32, name="vb")
         vc = const.tile([P, H], F32, name="vc")
@@ -135,75 +139,86 @@ def tile_nascell_w_kernel(
 
         acc = [bank("p47_%d" % c) for c in range(8)]
         for s in range(G_ALL):
-            wt = load_w(s, 4 * H, 4 * H)
+            wt = load_w(s, 4 * H, 4 * H, "quad", 6)
             for c in range(8):
                 mx_pass(acc[c][:], s, wt, BANK * c, 4 * H + BANK * c, BANK, 0, G_ALL - 1)
-        for h in range(2):
-            cols = slice(BANK * h, BANK * (h + 1))
-            nc.scalar.activation(out=va[:, cols], in_=acc[0 + h][:], func=ACT.Tanh)
-            nc.scalar.activation(out=vb[:, cols], in_=acc[2 + h][:], func=ACT.Sigmoid)
-            nc.scalar.activation(out=vc[:, cols], in_=acc[4 + h][:], func=ACT.Tanh)
-            nc.scalar.activation(out=vd[:, cols], in_=acc[6 + h][:], func=ACT.Sigmoid)
-        for h in range(2):
-            cols = slice(BANK * h, BANK * (h + 1))
-            nc.vector.tensor_tensor(out=va[:, cols], in0=va[:, cols], in1=vb[:, cols], op=ALU.mult)
-            nc.vector.tensor_tensor(out=vc[:, cols], in0=vc[:, cols], in1=vd[:, cols], op=ALU.add)
-            nc.scalar.activation(out=va[:, cols], in_=va[:, cols], func=ACT.Tanh)
-            nc.scalar.activation(out=vc[:, cols], in_=vc[:, cols], func=ACT.Sigmoid)
-            nc.vector.tensor_tensor(out=va[:, cols], in0=va[:, cols], in1=vc[:, cols], op=ALU.add)
-            nc.scalar.activation(out=va[:, cols], in_=va[:, cols], func=ACT.Tanh)
+        for i, (dst, func) in enumerate(((va, ACT.Tanh), (vb, ACT.Sigmoid), (vc, ACT.Tanh), (vd, ACT.Sigmoid))):
+            for h in range(2):
+                nc.scalar.activation(out=dst[:, half(h)], in_=acc[2 * i + h][:], func=func)
+        nc.vector.tensor_tensor(out=va[:], in0=va[:], in1=vb[:], op=ALU.mult)
+        nc.vector.tensor_tensor(out=vc[:], in0=vc[:], in1=vd[:], op=ALU.add)
+        nc.scalar.activation(out=va[:], in_=va[:], func=ACT.Tanh)
+        nc.scalar.activation(out=vc[:], in_=vc[:], func=ACT.Sigmoid)
+        nc.vector.tensor_tensor(out=va[:], in0=va[:], in1=vc[:], op=ALU.add)
+        nc.scalar.activation(out=va[:], in_=va[:], func=ACT.Tanh)
 
         nc.sync.dma_start(out=c_sb[:], in_=c_prev)
         acc = [bank("p01_%d" % c) for c in range(4)]
         for s in range(G_ALL):
-            wt = load_w(s, 0, 2 * H)
+            wt = load_w(s, 0, 2 * H, "pair", 6)
             for c in range(4):
                 mx_pass(acc[c][:], s, wt, BANK * c, BANK * c, BANK, 0, G_ALL - 1)
         for h in range(2):
-            cols = slice(BANK * h, BANK * (h + 1))
-            nc.scalar.activation(out=ve[:, cols], in_=acc[h][:], func=ACT.Sigmoid)
+            nc.scalar.activation(out=ve[:, half(h)], in_=acc[h][:], func=ACT.Sigmoid)
+        for h in range(2):
             nc.vector.scalar_tensor_tensor(
-                out=ve[:, cols], in0=acc[2 + h][:], scalar=0.0, in1=ve[:, cols], op0=ALU.max, op1=ALU.mult
+                out=ve[:, half(h)], in0=acc[2 + h][:], scalar=0.0, in1=ve[:, half(h)], op0=ALU.max, op1=ALU.mult
             )
-            nc.scalar.activation(out=ve[:, cols], in_=ve[:, cols], func=ACT.Tanh)
-            nc.vector.tensor_tensor(out=ve[:, cols], in0=ve[:, cols], in1=c_sb[:, cols], op=ALU.add)
-            nc.scalar.activation(out=ve[:, cols], in_=ve[:, cols], func=ACT.Tanh)
-            nc.vector.tensor_tensor(out=va[:, cols], in0=va[:, cols], in1=ve[:, cols], op=ALU.mult)
+        nc.scalar.activation(out=ve[:], in_=ve[:], func=ACT.Tanh)
+        nc.vector.tensor_tensor(out=ve[:], in0=ve[:], in1=c_sb[:], op=ALU.add)
+        nc.scalar.activation(out=ve[:], in_=ve[:], func=ACT.Tanh)
+        nc.vector.tensor_tensor(out=va[:], in0=va[:], in1=ve[:], op=ALU.mult)
 
-        chunks = [(0, 512), (512, 256), (768, 256)]
-        acc2 = [bank("p2_%d" % h) for h in range(2)]
-        accm = [bank("pm3_%d" % h) for h in range(2)]
-        for s in range(G_M):
-            wt = load_w(s, 2 * H, 2 * H)
+        acc2 = [bank("p2_%d" % j) for j in range(N_CH)]
+        acc3 = [bank("pm3_%d" % h) for h in range(2)]
+        for s in range(Z_FIRST):
+            if s == G_M:
+                for h in range(2):
+                    nc.vector.tensor_copy(out=vf[:, half(h)], in_=acc3[h][:])
+                acc3 = [bank("px3_%d" % h) for h in range(2)]
+            wt = load_w(s, 2 * H, 2 * H, "pair", 6)
+            for j in range(N_CH):
+                mx_pass(acc2[j][:, 0:CH], s, wt, CH * j, 2 * H + CH * j, CH, 0, G_ALL - 1)
             for h in range(2):
-                mx_pass(acc2[h][:], s, wt, BANK * h, 2 * H + BANK * h, BANK, 0, G_ALL - 1)
+                if s < G_M:
+                    mx_pass(acc3[h][:], s, wt, H + BANK * h, 3 * H + BANK * h, BANK, 0, G_M - 1)
+                else:
+                    mx_pass(acc3[h][:], s, wt, H + BANK * h, 3 * H + BANK * h, BANK, G_M, G_ALL - 1)
+        for s in range(Z_FIRST, G_ALL):
+            wt = load_w(s, 3 * H, H, "single", 3)
             for h in range(2):
-                mx_pass(accm[h][:], s, wt, H + BANK * h, 3 * H + BANK * h, BANK, 0, G_M - 1)
+                mx_pass(acc3[h][:], s, wt, BANK * h, 3 * H + BANK * h, BANK, G_M, G_ALL - 1)
         for h in range(2):
-            nc.vector.tensor_copy(out=vf[:, BANK * h : BANK * (h + 1)], in_=accm[h][:])
-        accx = [bank("px3_%d" % i) for i in range(len(chunks))]
-        for s in range(G_M, G_ALL - 1):
-            wt = load_w(s, 2 * H, 2 * H)
-            for h in range(2):
-                mx_pass(acc2[h][:], s, wt, BANK * h, 2 * H + BANK * h, BANK, 0, G_ALL - 1)
-            for i, (c0, n) in enumerate(chunks):
-                mx_pass(accx[i][:, 0:n], s, wt, H + c0, 3 * H + c0, n, G_M, G_ALL - 1)
-        s = G_ALL - 1
-        wt = load_w(s, 2 * H, H)
-        for h in range(2):
-            mx_pass(acc2[h][:], s, wt, BANK * h, 2 * H + BANK * h, BANK, 0, G_ALL - 1)
-            nc.scalar.activation(out=vg[:, BANK * h : BANK * (h + 1)], in_=acc2[h][:], func=ACT.Sigmoid)
-        for i, (c0, n) in enumerate(chunks):
-            cols = slice(c0, c0 + n)
-            wt = load_w(s, 3 * H + c0, n)
-            mx_pass(accx[i][:, 0:n], s, wt, 0, 3 * H + c0, n, G_M, G_ALL - 1)
-            nc.vector.tensor_tensor(out=vf[:, cols], in0=accx[i][:, 0:n], in1=vf[:, cols], op=ALU.mult)
+            nc.vector.tensor_tensor(out=vf[:, half(h)], in0=acc3[h][:], in1=vf[:, half(h)], op=ALU.mult)
+
+        n_z = G_ALL - Z_FIRST
+
+        def finish(j):
+            cols = slice(CH * j, CH * (j + 1))
+            nc.scalar.activation(out=va[:, cols], in_=va[:, cols], func=ACT.Tanh)
+            nc.sync.dma_start(out=out_0[:, cols], in_=va[:, cols])
+            nc.vector.tensor_tensor(out=ve[:, cols], in0=ve[:, cols], in1=vg[:, cols], op=ALU.mult)
+            nc.sync.dma_start(out=out_1[:, cols], in_=ve[:, cols])
+
+        z_tiles = []
+        for j in range(N_CH):
+            wt = wpool.tile([P, n_z * CH], U32, tag="chunk", bufs=N_CH, name="wz%d" % j, align_bytes=64)
+            lo = 2 * H + CH * j
+            nc.sync.dma_start(
+                out=wt[:].bitcast(I32).rearrange("p (s n) -> p s n", s=n_z),
+                in_=wi_words[Z_FIRST - G_M :, :, lo : lo + CH].rearrange("s p n -> p s n"),
+            )
+            z_tiles.append(wt)
+        for j in range(N_CH):
+            cols = slice(CH * j, CH * (j + 1))
+            for s in range(Z_FIRST, G_ALL):
+                mx_pass(acc2[j][:, 0:CH], s, z_tiles[j], CH * (s - Z_FIRST), 2 * H + CH * j, CH, 0, G_ALL - 1)
+            nc.scalar.activation(out=vg[:, cols], in_=acc2[j][:, 0:CH], func=ACT.Sigmoid)
             nc.vector.scalar_tensor_tensor(
                 out=vg[:, cols], in0=vf[:, cols], scalar=0.0, in1=vg[:, cols], op0=ALU.max, op1=ALU.add
             )
+            if j > 0:
+                finish(j - 1)
             nc.scalar.activation(out=vg[:, cols], in_=vg[:, cols], func=ACT.Tanh)
             nc.vector.tensor_tensor(out=va[:, cols], in0=va[:, cols], in1=vg[:, cols], op=ALU.mult)
-            nc.vector.tensor_tensor(out=ve[:, cols], in0=ve[:, cols], in1=vg[:, cols], op=ALU.mult)
-            nc.scalar.activation(out=va[:, cols], in_=va[:, cols], func=ACT.Tanh)
-            nc.sync.dma_start(out=out_1[:, cols], in_=ve[:, cols])
-            nc.sync.dma_start(out=out_0[:, cols], in_=va[:, cols])
+        finish(N_CH - 1)

@@ -32,7 +32,7 @@ def tile_nascell_w_kernel(
     wm_words = w_m_words.rearrange("g p n t -> g p (n t)").bitcast(I32)
     wi_words = w_inputs_words.rearrange("g p n t -> g p (n t)").bitcast(I32)
     wm_scales = w_m_scales.bitcast(I32)
-    wi_scales = w_inputs_scales.bitcast(I32)
+    wi_scales_f = w_inputs_scales.bitcast(F32)
 
     with ExitStack() as ctx:
         const = ctx.enter_context(tc.tile_pool(name="const", bufs=1))
@@ -58,17 +58,19 @@ def tile_nascell_w_kernel(
         ident = const.tile([P, P], F32, name="ident")
         masks.make_identity(nc, ident[:])
 
-        for g in range(G_M):
+        def load_m_planes(g):
             for q in range(4):
                 nc.sync.dma_start(
                     out=planes_m[32 * q : 32 * q + 16, 2048 * g : 2048 * (g + 1)].bitcast(I32),
                     in_=wm_scales[g, 4 * q : 4 * q + 4, :].rearrange("r (j n) -> j r n", j=4),
                 )
-        for q in range(4):
-            nc.sync.dma_start(
-                out=planes_x[32 * q : 32 * q + 16, :].bitcast(I32),
-                in_=wi_scales[:, 4 * q : 4 * q + 4, :],
-            )
+
+        for r in range(4):
+            for q in (0, 2, 1, 3):
+                nc.gpsimd.dma_start(
+                    out=planes_x[32 * q + r : 32 * q + 16 : 4, :].bitcast(F32),
+                    in_=wi_scales_f[:, 4 * q + r, :],
+                )
 
         grouped = const.tile([P, G_ALL * 512], BF16, name="grouped", align_bytes=64)
         grouped_w = grouped[:].bitcast(F32).rearrange("p (s b u) -> p s b u", s=G_ALL, u=2)
@@ -140,6 +142,8 @@ def tile_nascell_w_kernel(
         acc = [bank("p47_%d" % c) for c in range(8)]
         for s in range(G_ALL):
             wt = load_w(s, 4 * H, 4 * H, "quad", 6)
+            if s < G_M:
+                load_m_planes(s)
             for c in range(8):
                 mx_pass(acc[c][:], s, wt, BANK * c, 4 * H + BANK * c, BANK, 0, G_ALL - 1)
         for i, (dst, func) in enumerate(((va, ACT.Tanh), (vb, ACT.Sigmoid), (vc, ACT.Tanh), (vd, ACT.Sigmoid))):

@@ -32,7 +32,7 @@ def tile_nascell_w_kernel(
     wm_words = w_m_words.rearrange("g p n t -> g p (n t)").bitcast(I32)
     wi_words = w_inputs_words.rearrange("g p n t -> g p (n t)").bitcast(I32)
     wm_scales = w_m_scales.bitcast(I32)
-    wi_scales_f = w_inputs_scales.bitcast(F32)
+    wi_scales = w_inputs_scales.bitcast(I32)
 
     with ExitStack() as ctx:
         const = ctx.enter_context(tc.tile_pool(name="const", bufs=1))
@@ -48,8 +48,8 @@ def tile_nascell_w_kernel(
 
         planes_m = const.tile([P, G_M * 2048], U8, name="planes_m", align_bytes=64)
         planes_x = const.tile([P, 8 * H], U8, name="planes_x", align_bytes=64)
-        nc.vector.memset(planes_m[:].bitcast(I32), 0)
         nc.vector.memset(planes_x[:].bitcast(I32), 0)
+        nc.vector.memset(planes_m[:].bitcast(I32), 0)
 
         warm = const.tile([P, 16], F32, name="warm")
         nc.vector.memset(warm[:], 0.0)
@@ -58,18 +58,17 @@ def tile_nascell_w_kernel(
         ident = const.tile([P, P], F32, name="ident")
         masks.make_identity(nc, ident[:])
 
-        def load_m_planes(g):
-            for q in range(4):
+        for h in range(2):
+            for q in (0, 2, 1, 3):
+                nc.sync.dma_start(
+                    out=planes_x[32 * q : 32 * q + 16, 4096 * h : 4096 * (h + 1)].bitcast(I32),
+                    in_=wi_scales[:, 4 * q : 4 * q + 4, 1024 * h : 1024 * (h + 1)],
+                )
+        for g in range(G_M):
+            for q in (0, 2, 1, 3):
                 nc.sync.dma_start(
                     out=planes_m[32 * q : 32 * q + 16, 2048 * g : 2048 * (g + 1)].bitcast(I32),
                     in_=wm_scales[g, 4 * q : 4 * q + 4, :].rearrange("r (j n) -> j r n", j=4),
-                )
-
-        for r in range(4):
-            for q in (0, 2, 1, 3):
-                nc.gpsimd.dma_start(
-                    out=planes_x[32 * q + r : 32 * q + 16 : 4, :].bitcast(F32),
-                    in_=wi_scales_f[:, 4 * q + r, :],
                 )
 
         grouped = const.tile([P, G_ALL * 512], BF16, name="grouped", align_bytes=64)
@@ -142,8 +141,6 @@ def tile_nascell_w_kernel(
         acc = [bank("p47_%d" % c) for c in range(8)]
         for s in range(G_ALL):
             wt = load_w(s, 4 * H, 4 * H, "quad", 6)
-            if s < G_M:
-                load_m_planes(s)
             for c in range(8):
                 mx_pass(acc[c][:], s, wt, BANK * c, 4 * H + BANK * c, BANK, 0, G_ALL - 1)
         for i, (dst, func) in enumerate(((va, ACT.Tanh), (vb, ACT.Sigmoid), (vc, ACT.Tanh), (vd, ACT.Sigmoid))):

@@ -194,13 +194,6 @@ def tile_nascell_w_kernel(
 
         n_z = G_ALL - Z_FIRST
 
-        def finish(j):
-            cols = slice(CH * j, CH * (j + 1))
-            nc.scalar.activation(out=va[:, cols], in_=va[:, cols], func=ACT.Tanh)
-            nc.sync.dma_start(out=out_0[:, cols], in_=va[:, cols])
-            nc.vector.tensor_tensor(out=ve[:, cols], in0=ve[:, cols], in1=vg[:, cols], op=ALU.mult)
-            nc.sync.dma_start(out=out_1[:, cols], in_=ve[:, cols])
-
         z_tiles = []
         for j in range(N_CH):
             wt = wpool.tile([P, n_z * CH], U32, tag="chunk", bufs=N_CH, name="wz%d" % j, align_bytes=64)
@@ -210,16 +203,25 @@ def tile_nascell_w_kernel(
                 in_=wi_words[Z_FIRST - G_M :, :, lo : lo + CH].rearrange("s p n -> p s n"),
             )
             z_tiles.append(wt)
-        for j in range(N_CH):
-            cols = slice(CH * j, CH * (j + 1))
-            for s in range(Z_FIRST, G_ALL):
-                mx_pass(acc2[j][:, 0:CH], s, z_tiles[j], CH * (s - Z_FIRST), 2 * H + CH * j, CH, 0, G_ALL - 1)
-            nc.scalar.activation(out=vg[:, cols], in_=acc2[j][:, 0:CH], func=ACT.Sigmoid)
-            nc.vector.scalar_tensor_tensor(
-                out=vg[:, cols], in0=vf[:, cols], scalar=0.0, in1=vg[:, cols], op0=ALU.max, op1=ALU.add
-            )
-            if j > 0:
-                finish(j - 1)
-            nc.scalar.activation(out=vg[:, cols], in_=vg[:, cols], func=ACT.Tanh)
-            nc.vector.tensor_tensor(out=va[:, cols], in0=va[:, cols], in1=vg[:, cols], op=ALU.mult)
-        finish(N_CH - 1)
+        def chunk(j):
+            return slice(CH * j, CH * (j + 1))
+
+        for step in range(N_CH + 2):
+            if step < N_CH:
+                j = step
+                for s in range(Z_FIRST, G_ALL):
+                    mx_pass(acc2[j][:, 0:CH], s, z_tiles[j], CH * (s - Z_FIRST), 2 * H + CH * j, CH, 0, G_ALL - 1)
+                nc.scalar.activation(out=vg[:, chunk(j)], in_=acc2[j][:, 0:CH], func=ACT.Sigmoid)
+                nc.vector.scalar_tensor_tensor(
+                    out=vg[:, chunk(j)], in0=vf[:, chunk(j)], scalar=0.0, in1=vg[:, chunk(j)], op0=ALU.max, op1=ALU.add
+                )
+            if 1 <= step <= N_CH:
+                j = step - 1
+                nc.scalar.activation(out=vg[:, chunk(j)], in_=vg[:, chunk(j)], func=ACT.Tanh)
+                nc.vector.tensor_tensor(out=va[:, chunk(j)], in0=va[:, chunk(j)], in1=vg[:, chunk(j)], op=ALU.mult)
+            if step >= 2:
+                j = step - 2
+                nc.scalar.activation(out=va[:, chunk(j)], in_=va[:, chunk(j)], func=ACT.Tanh)
+                nc.sync.dma_start(out=out_0[:, chunk(j)], in_=va[:, chunk(j)])
+                nc.vector.tensor_tensor(out=ve[:, chunk(j)], in0=ve[:, chunk(j)], in1=vg[:, chunk(j)], op=ALU.mult)
+                nc.sync.dma_start(out=out_1[:, chunk(j)], in_=ve[:, chunk(j)])

@@ -100,10 +100,13 @@ def tile_nascell_w_kernel(
             in_=grouped[:, G_M * 512 :],
         )
 
-        def load_w(s, n0, n, tag, bufs):
-            wt = wpool.tile([P, n], U32, tag=tag, bufs=bufs, name="w%d_%d" % (s, n0), align_bytes=64)
-            src = wm_words[s] if s < G_M else wi_words[s - G_M]
-            nc.sync.dma_start(out=wt[:].bitcast(I32), in_=src[:, n0 : n0 + n])
+        def load_w(s, count, n0, n, tag, bufs):
+            wt = wpool.tile([P, count * n], U32, tag=tag, bufs=bufs, name="w%d_%d" % (s, n0), align_bytes=64)
+            src = wm_words[s : s + count] if s < G_M else wi_words[s - G_M : s - G_M + count]
+            nc.sync.dma_start(
+                out=wt[:].bitcast(I32).rearrange("p (s n) -> p s n", s=count),
+                in_=src[:, :, n0 : n0 + n].rearrange("s p n -> p s n"),
+            )
             return wt
 
         def plane(s, n0, n):
@@ -139,10 +142,12 @@ def tile_nascell_w_kernel(
         vg = const.tile([P, H], F32, name="vg")
 
         acc = [bank("p47_%d" % c) for c in range(8)]
-        for s in range(G_ALL):
-            wt = load_w(s, 4 * H, 4 * H, "quad", 6)
-            for c in range(8):
-                mx_pass(acc[c][:], s, wt, BANK * c, 4 * H + BANK * c, BANK, 0, G_ALL - 1)
+        for s0 in range(0, G_ALL, 2):
+            wt = load_w(s0, 2, 4 * H, 4 * H, "quads", 3)
+            for s in (s0, s0 + 1):
+                for c in range(8):
+                    off = 4 * H * (s - s0) + BANK * c
+                    mx_pass(acc[c][:], s, wt, off, 4 * H + BANK * c, BANK, 0, G_ALL - 1)
         for i, (dst, func) in enumerate(((va, ACT.Tanh), (vb, ACT.Sigmoid), (vc, ACT.Tanh), (vd, ACT.Sigmoid))):
             for h in range(2):
                 nc.scalar.activation(out=dst[:, half(h)], in_=acc[2 * i + h][:], func=func)
@@ -155,10 +160,12 @@ def tile_nascell_w_kernel(
 
         nc.sync.dma_start(out=c_sb[:], in_=c_prev)
         acc = [bank("p01_%d" % c) for c in range(4)]
-        for s in range(G_ALL):
-            wt = load_w(s, 0, 2 * H, "pair", 6)
-            for c in range(4):
-                mx_pass(acc[c][:], s, wt, BANK * c, BANK * c, BANK, 0, G_ALL - 1)
+        for s0 in range(0, G_ALL, 2):
+            wt = load_w(s0, 2, 0, 2 * H, "pairs", 3)
+            for s in (s0, s0 + 1):
+                for c in range(4):
+                    off = 2 * H * (s - s0) + BANK * c
+                    mx_pass(acc[c][:], s, wt, off, BANK * c, BANK, 0, G_ALL - 1)
         for h in range(2):
             nc.scalar.activation(out=ve[:, half(h)], in_=acc[h][:], func=ACT.Sigmoid)
         for h in range(2):
@@ -172,23 +179,26 @@ def tile_nascell_w_kernel(
 
         acc2 = [bank("p2_%d" % j) for j in range(N_CH)]
         acc3 = [bank("pm3_%d" % h) for h in range(2)]
+        wt_m = load_w(0, G_M, 2 * H, 2 * H, "pairs", 3)
+        wt_x = load_w(G_M, 1, 2 * H, 2 * H, "pairs", 3)
         for s in range(Z_FIRST):
             if s == G_M:
                 for h in range(2):
                     nc.vector.tensor_copy(out=vf[:, half(h)], in_=acc3[h][:])
                 acc3 = [bank("px3_%d" % h) for h in range(2)]
-            wt = load_w(s, 2 * H, 2 * H, "pair", 6)
+            wt, off = (wt_m, 2 * H * s) if s < G_M else (wt_x, 0)
             for j in range(N_CH):
-                mx_pass(acc2[j][:, 0:CH], s, wt, CH * j, 2 * H + CH * j, CH, 0, G_ALL - 1)
+                mx_pass(acc2[j][:, 0:CH], s, wt, off + CH * j, 2 * H + CH * j, CH, 0, G_ALL - 1)
             for h in range(2):
                 if s < G_M:
-                    mx_pass(acc3[h][:], s, wt, H + BANK * h, 3 * H + BANK * h, BANK, 0, G_M - 1)
+                    mx_pass(acc3[h][:], s, wt, off + H + BANK * h, 3 * H + BANK * h, BANK, 0, G_M - 1)
                 else:
-                    mx_pass(acc3[h][:], s, wt, H + BANK * h, 3 * H + BANK * h, BANK, G_M, G_ALL - 1)
+                    mx_pass(acc3[h][:], s, wt, off + H + BANK * h, 3 * H + BANK * h, BANK, G_M, G_ALL - 1)
+        wt = load_w(Z_FIRST, G_ALL - Z_FIRST, 3 * H, H, "singles", 1)
         for s in range(Z_FIRST, G_ALL):
-            wt = load_w(s, 3 * H, H, "single", 3)
             for h in range(2):
-                mx_pass(acc3[h][:], s, wt, BANK * h, 3 * H + BANK * h, BANK, G_M, G_ALL - 1)
+                off = H * (s - Z_FIRST) + BANK * h
+                mx_pass(acc3[h][:], s, wt, off, 3 * H + BANK * h, BANK, G_M, G_ALL - 1)
         for h in range(2):
             nc.vector.tensor_tensor(out=vf[:, half(h)], in0=acc3[h][:], in1=vf[:, half(h)], op=ALU.mult)
 

@@ -58,14 +58,12 @@ def tile_nascell_w_kernel(
         ident = const.tile([P, P], F32, name="ident")
         masks.make_identity(nc, ident[:])
 
-        for h in range(2):
-            for q in (0, 2, 1, 3):
-                nc.sync.dma_start(
-                    out=planes_x[32 * q : 32 * q + 16, 4096 * h : 4096 * (h + 1)].bitcast(I32),
-                    in_=wi_scales[:, 4 * q : 4 * q + 4, 1024 * h : 1024 * (h + 1)],
-                )
-        for g in range(G_M):
-            for q in (0, 2, 1, 3):
+        for q in (0, 2, 1, 3):
+            nc.sync.dma_start(
+                out=planes_x[32 * q : 32 * q + 16, :].bitcast(I32),
+                in_=wi_scales[:, 4 * q : 4 * q + 4, :],
+            )
+            for g in range(G_M):
                 nc.sync.dma_start(
                     out=planes_m[32 * q : 32 * q + 16, 2048 * g : 2048 * (g + 1)].bitcast(I32),
                     in_=wm_scales[g, 4 * q : 4 * q + 4, :].rearrange("r (j n) -> j r n", j=4),
@@ -179,26 +177,26 @@ def tile_nascell_w_kernel(
 
         acc2 = [bank("p2_%d" % j) for j in range(N_CH)]
         acc3 = [bank("pm3_%d" % h) for h in range(2)]
-        wt_m = load_w(0, G_M, 2 * H, 2 * H, "pairs", 3)
-        wt_x = load_w(G_M, 1, 2 * H, 2 * H, "pairs", 3)
-        for s in range(Z_FIRST):
-            if s == G_M:
-                for h in range(2):
-                    nc.vector.tensor_copy(out=vf[:, half(h)], in_=acc3[h][:])
-                acc3 = [bank("px3_%d" % h) for h in range(2)]
-            wt, off = (wt_m, 2 * H * s) if s < G_M else (wt_x, 0)
+        wt = load_w(0, G_M, 2 * H, 2 * H, "pairs", 3)
+        for s in range(G_M):
+            off = 2 * H * s
             for j in range(N_CH):
                 mx_pass(acc2[j][:, 0:CH], s, wt, off + CH * j, 2 * H + CH * j, CH, 0, G_ALL - 1)
             for h in range(2):
-                if s < G_M:
-                    mx_pass(acc3[h][:], s, wt, off + H + BANK * h, 3 * H + BANK * h, BANK, 0, G_M - 1)
-                else:
-                    mx_pass(acc3[h][:], s, wt, off + H + BANK * h, 3 * H + BANK * h, BANK, G_M, G_ALL - 1)
-        wt = load_w(Z_FIRST, G_ALL - Z_FIRST, 3 * H, H, "singles", 1)
-        for s in range(Z_FIRST, G_ALL):
+                mx_pass(acc3[h][:], s, wt, off + H + BANK * h, 3 * H + BANK * h, BANK, 0, G_M - 1)
+        for h in range(2):
+            nc.vector.tensor_copy(out=vf[:, half(h)], in_=acc3[h][:])
+        acc3 = [bank("px3_%d" % h) for h in range(2)]
+        wt = load_w(G_M, G_X, 3 * H, H, "pairs", 3)
+        for s in range(G_M, G_ALL):
             for h in range(2):
-                off = H * (s - Z_FIRST) + BANK * h
+                off = H * (s - G_M) + BANK * h
                 mx_pass(acc3[h][:], s, wt, off, 3 * H + BANK * h, BANK, G_M, G_ALL - 1)
+        wt = load_w(G_M, Z_FIRST - G_M, 2 * H, H, "first", 1)
+        for s in range(G_M, Z_FIRST):
+            for j in range(N_CH):
+                off = H * (s - G_M) + CH * j
+                mx_pass(acc2[j][:, 0:CH], s, wt, off, 2 * H + CH * j, CH, 0, G_ALL - 1)
         for h in range(2):
             nc.vector.tensor_tensor(out=vf[:, half(h)], in0=acc3[h][:], in1=vf[:, half(h)], op=ALU.mult)
 

@@ -58,16 +58,18 @@ def tile_nascell_w_kernel(
         ident = const.tile([P, P], F32, name="ident")
         masks.make_identity(nc, ident[:])
 
-        for q in (0, 2, 1, 3):
-            nc.sync.dma_start(
-                out=planes_x[32 * q : 32 * q + 16, :].bitcast(I32),
-                in_=wi_scales[:, 4 * q : 4 * q + 4, :],
-            )
-            for g in range(G_M):
+        for quadrants in ((2, 3), (0, 1)):
+            for q in quadrants:
                 nc.sync.dma_start(
-                    out=planes_m[32 * q : 32 * q + 16, 2048 * g : 2048 * (g + 1)].bitcast(I32),
-                    in_=wm_scales[g, 4 * q : 4 * q + 4, :].rearrange("r (j n) -> j r n", j=4),
+                    out=planes_x[32 * q : 32 * q + 16, :].bitcast(I32),
+                    in_=wi_scales[:, 4 * q : 4 * q + 4, :],
                 )
+            for q in quadrants:
+                for g in range(G_M):
+                    nc.sync.dma_start(
+                        out=planes_m[32 * q : 32 * q + 16, 2048 * g : 2048 * (g + 1)].bitcast(I32),
+                        in_=wm_scales[g, 4 * q : 4 * q + 4, :].rearrange("r (j n) -> j r n", j=4),
+                    )
 
         grouped = const.tile([P, G_ALL * 512], BF16, name="grouped", align_bytes=64)
         grouped_w = grouped[:].bitcast(F32).rearrange("p (s b u) -> p s b u", s=G_ALL, u=2)

@@ -19,8 +19,9 @@ G_X = 4
 G_ALL = G_M + G_X
 BANK = 512
 CH = 256
-N_CH = H // CH
-Z_FIRST = 3
+PARTS = ((0, 256), (256, 256), (512, 256), (768, 128), (896, 128))
+STEPS = ((0,), (1,), (2,), (3, 4))
+N_ST = len(STEPS)
 
 FLOPS = 2 * 128 * (1024 + 2048) * 8192
 
@@ -142,28 +143,36 @@ def tile_nascell_w_kernel(
         vg = const.tile([P, H], F32, name="vg")
 
         acc = [bank("p47_%d" % c) for c in range(8)]
-        for s0 in range(0, G_ALL, 2):
-            wt = load_w(s0, 2, 4 * H, 4 * H, "quads", 3)
-            for s in (s0, s0 + 1):
-                for c in range(8):
+        order47 = (0, 2, 1, 3, 4, 6, 5, 7)
+        for s0, count, tag in ((0, G_M, "w32k"), (G_M, G_X, "w64k")):
+            wt = load_w(s0, count, 4 * H, 4 * H, tag, 2 if tag == "w32k" else 1)
+            for c in order47:
+                for s in range(s0, s0 + count):
                     off = 4 * H * (s - s0) + BANK * c
                     mx_pass(acc[c][:], s, wt, off, 4 * H + BANK * c, BANK, 0, G_ALL - 1)
-        for i, (dst, func) in enumerate(((va, ACT.Tanh), (vb, ACT.Sigmoid), (vc, ACT.Tanh), (vd, ACT.Sigmoid))):
-            for h in range(2):
-                nc.scalar.activation(out=dst[:, half(h)], in_=acc[2 * i + h][:], func=func)
-        nc.vector.tensor_tensor(out=va[:], in0=va[:], in1=vb[:], op=ALU.mult)
-        nc.vector.tensor_tensor(out=vc[:], in0=vc[:], in1=vd[:], op=ALU.add)
+        dst47 = (va, vb, vc, vd)
+        func47 = (ACT.Tanh, ACT.Sigmoid, ACT.Tanh, ACT.Sigmoid)
+        for c in order47:
+            nc.scalar.activation(out=dst47[c // 2][:, half(c % 2)], in_=acc[c][:], func=func47[c // 2])
+        for h in range(2):
+            nc.vector.tensor_tensor(out=va[:, half(h)], in0=va[:, half(h)], in1=vb[:, half(h)], op=ALU.mult)
+        for h in range(2):
+            nc.vector.tensor_tensor(out=vc[:, half(h)], in0=vc[:, half(h)], in1=vd[:, half(h)], op=ALU.add)
         nc.scalar.activation(out=va[:], in_=va[:], func=ACT.Tanh)
-        nc.scalar.activation(out=vc[:], in_=vc[:], func=ACT.Sigmoid)
-        nc.vector.tensor_tensor(out=va[:], in0=va[:], in1=vc[:], op=ALU.add)
-        nc.scalar.activation(out=va[:], in_=va[:], func=ACT.Tanh)
+        for h in range(2):
+            nc.scalar.activation(out=vc[:, half(h)], in_=vc[:, half(h)], func=ACT.Sigmoid)
+        for h in range(2):
+            nc.vector.tensor_tensor(out=va[:, half(h)], in0=va[:, half(h)], in1=vc[:, half(h)], op=ALU.add)
+        for h in range(2):
+            nc.scalar.activation(out=va[:, half(h)], in_=va[:, half(h)], func=ACT.Tanh)
 
         nc.sync.dma_start(out=c_sb[:], in_=c_prev)
         acc = [bank("p01_%d" % c) for c in range(4)]
-        for s0 in range(0, G_ALL, 2):
-            wt = load_w(s0, 2, 0, 2 * H, "pairs", 3)
-            for s in (s0, s0 + 1):
-                for c in range(4):
+        order01 = (0, 2, 1, 3)
+        for s0, count, tag in ((0, G_M, "w16k"), (G_M, G_X, "w32k")):
+            wt = load_w(s0, count, 0, 2 * H, tag, 2)
+            for c in order01:
+                for s in range(s0, s0 + count):
                     off = 2 * H * (s - s0) + BANK * c
                     mx_pass(acc[c][:], s, wt, off, BANK * c, BANK, 0, G_ALL - 1)
         for h in range(2):
@@ -172,66 +181,67 @@ def tile_nascell_w_kernel(
             nc.vector.scalar_tensor_tensor(
                 out=ve[:, half(h)], in0=acc[2 + h][:], scalar=0.0, in1=ve[:, half(h)], op0=ALU.max, op1=ALU.mult
             )
-        nc.scalar.activation(out=ve[:], in_=ve[:], func=ACT.Tanh)
-        nc.vector.tensor_tensor(out=ve[:], in0=ve[:], in1=c_sb[:], op=ALU.add)
-        nc.scalar.activation(out=ve[:], in_=ve[:], func=ACT.Tanh)
-        nc.vector.tensor_tensor(out=va[:], in0=va[:], in1=ve[:], op=ALU.mult)
-
-        acc2 = [bank("p2_%d" % j) for j in range(N_CH)]
-        acc3 = [bank("pm3_%d" % h) for h in range(2)]
-        wt = load_w(0, G_M, 2 * H, 2 * H, "pairs", 3)
-        for s in range(G_M):
-            off = 2 * H * s
-            for j in range(N_CH):
-                mx_pass(acc2[j][:, 0:CH], s, wt, off + CH * j, 2 * H + CH * j, CH, 0, G_ALL - 1)
-            for h in range(2):
-                mx_pass(acc3[h][:], s, wt, off + H + BANK * h, 3 * H + BANK * h, BANK, 0, G_M - 1)
         for h in range(2):
-            nc.vector.tensor_copy(out=vf[:, half(h)], in_=acc3[h][:])
-        acc3 = [bank("px3_%d" % h) for h in range(2)]
-        wt = load_w(G_M, G_X, 3 * H, H, "pairs", 3)
-        for s in range(G_M, G_ALL):
-            for h in range(2):
+            nc.scalar.activation(out=ve[:, half(h)], in_=ve[:, half(h)], func=ACT.Tanh)
+
+        acc_m3 = [bank("pm3_%d" % h) for h in range(2)]
+        acc_x3 = [bank("px3_%d" % h) for h in range(2)]
+        acc2 = [bank("p2_%d" % i) for i in range(len(PARTS))]
+        wt = load_w(0, G_M, 2 * H, 2 * H, "w16k", 2)
+        for h in range(2):
+            for s in range(G_M):
+                mx_pass(acc_m3[h][:], s, wt, 2 * H * s + H + BANK * h, 3 * H + BANK * h, BANK, 0, G_M - 1)
+        for i, (lo, n) in enumerate(PARTS):
+            for s in range(G_M):
+                mx_pass(acc2[i][:, 0:n], s, wt, 2 * H * s + lo, 2 * H + lo, n, 0, G_ALL - 1)
+        for h in range(2):
+            nc.vector.tensor_copy(out=vf[:, half(h)], in_=acc_m3[h][:])
+        for h in range(2):
+            nc.vector.tensor_tensor(out=ve[:, half(h)], in0=ve[:, half(h)], in1=c_sb[:, half(h)], op=ALU.add)
+        for h in range(2):
+            nc.scalar.activation(out=ve[:, half(h)], in_=ve[:, half(h)], func=ACT.Tanh)
+        for h in range(2):
+            nc.vector.tensor_tensor(out=va[:, half(h)], in0=va[:, half(h)], in1=ve[:, half(h)], op=ALU.mult)
+        wt = load_w(G_M, G_X, 3 * H, H, "w64k", 1)
+        for h in range(2):
+            for s in range(G_M, G_ALL):
                 off = H * (s - G_M) + BANK * h
-                mx_pass(acc3[h][:], s, wt, off, 3 * H + BANK * h, BANK, G_M, G_ALL - 1)
-        wt = load_w(G_M, Z_FIRST - G_M, 2 * H, H, "first", 1)
-        for s in range(G_M, Z_FIRST):
-            for j in range(N_CH):
-                off = H * (s - G_M) + CH * j
-                mx_pass(acc2[j][:, 0:CH], s, wt, off, 2 * H + CH * j, CH, 0, G_ALL - 1)
-        for h in range(2):
-            nc.vector.tensor_tensor(out=vf[:, half(h)], in0=acc3[h][:], in1=vf[:, half(h)], op=ALU.mult)
-
-        n_z = G_ALL - Z_FIRST
+                mx_pass(acc_x3[h][:], s, wt, off, 3 * H + BANK * h, BANK, G_M, G_ALL - 1)
+            nc.vector.tensor_tensor(out=vf[:, half(h)], in0=acc_x3[h][:], in1=vf[:, half(h)], op=ALU.mult)
 
         z_tiles = []
-        for j in range(N_CH):
-            wt = wpool.tile([P, n_z * CH], U32, tag="chunk", bufs=N_CH, name="wz%d" % j, align_bytes=64)
-            lo = 2 * H + CH * j
-            nc.sync.dma_start(
-                out=wt[:].bitcast(I32).rearrange("p (s n) -> p s n", s=n_z),
-                in_=wi_words[Z_FIRST - G_M :, :, lo : lo + CH].rearrange("s p n -> p s n"),
-            )
-            z_tiles.append(wt)
-        def chunk(j):
-            return slice(CH * j, CH * (j + 1))
+        for lo, n, tag, bufs in ((0, BANK, "w32k", 2), (BANK, CH, "w4k", 2), (BANK + CH, CH, "w4k", 2)):
+            wt = load_w(G_M, G_X, 2 * H + lo, n, tag, bufs)
+            for j in range(n // CH):
+                z_tiles.append((wt, lo, n))
 
-        for step in range(N_CH + 2):
-            if step < N_CH:
-                j = step
-                for s in range(Z_FIRST, G_ALL):
-                    mx_pass(acc2[j][:, 0:CH], s, z_tiles[j], CH * (s - Z_FIRST), 2 * H + CH * j, CH, 0, G_ALL - 1)
-                nc.scalar.activation(out=vg[:, chunk(j)], in_=acc2[j][:, 0:CH], func=ACT.Sigmoid)
-                nc.vector.scalar_tensor_tensor(
-                    out=vg[:, chunk(j)], in0=vf[:, chunk(j)], scalar=0.0, in1=vg[:, chunk(j)], op0=ALU.max, op1=ALU.add
-                )
-            if 1 <= step <= N_CH:
-                j = step - 1
-                nc.scalar.activation(out=vg[:, chunk(j)], in_=vg[:, chunk(j)], func=ACT.Tanh)
-                nc.vector.tensor_tensor(out=va[:, chunk(j)], in0=va[:, chunk(j)], in1=vg[:, chunk(j)], op=ALU.mult)
+        def cols(i):
+            lo, n = PARTS[i]
+            return slice(lo, lo + n)
+
+        for step in range(N_ST + 2):
+            if step < N_ST:
+                wt, w_lo, w_n = z_tiles[step]
+                for i in STEPS[step]:
+                    lo, n = PARTS[i]
+                    for s in range(G_M, G_ALL):
+                        off = w_n * (s - G_M) + lo - w_lo
+                        mx_pass(acc2[i][:, 0:n], s, wt, off, 2 * H + lo, n, 0, G_ALL - 1)
+                    nc.scalar.activation(out=vg[:, cols(i)], in_=acc2[i][:, 0:n], func=ACT.Sigmoid)
+                for i in STEPS[step]:
+                    nc.vector.scalar_tensor_tensor(
+                        out=vg[:, cols(i)], in0=vf[:, cols(i)], scalar=0.0, in1=vg[:, cols(i)], op0=ALU.max, op1=ALU.add
+                    )
+            if 1 <= step <= N_ST:
+                for i in STEPS[step - 1]:
+                    nc.scalar.activation(out=vg[:, cols(i)], in_=vg[:, cols(i)], func=ACT.Tanh)
+                for i in STEPS[step - 1]:
+                    nc.vector.tensor_tensor(out=va[:, cols(i)], in0=va[:, cols(i)], in1=vg[:, cols(i)], op=ALU.mult)
             if step >= 2:
-                j = step - 2
-                nc.scalar.activation(out=va[:, chunk(j)], in_=va[:, chunk(j)], func=ACT.Tanh)
-                nc.sync.dma_start(out=out_0[:, chunk(j)], in_=va[:, chunk(j)])
-                nc.vector.tensor_tensor(out=ve[:, chunk(j)], in0=ve[:, chunk(j)], in1=vg[:, chunk(j)], op=ALU.mult)
-                nc.sync.dma_start(out=out_1[:, chunk(j)], in_=ve[:, chunk(j)])
+                for i in STEPS[step - 2]:
+                    nc.scalar.activation(out=va[:, cols(i)], in_=va[:, cols(i)], func=ACT.Tanh)
+                for i in STEPS[step - 2]:
+                    nc.vector.tensor_tensor(out=ve[:, cols(i)], in0=ve[:, cols(i)], in1=vg[:, cols(i)], op=ALU.mult)
+                whole = slice(CH * (step - 2), CH * (step - 1))
+                nc.sync.dma_start(out=out_1[:, whole], in_=ve[:, whole])
+                nc.sync.dma_start(out=out_0[:, whole], in_=va[:, whole])

@@ -18,10 +18,7 @@ G_M = 2
 G_X = 4
 G_ALL = G_M + G_X
 BANK = 512
-CH = 256
-PARTS = ((0, 256), (256, 256), (512, 256), (768, 128), (896, 128))
-STEPS = ((0,), (1,), (2,), (3, 4))
-N_ST = len(STEPS)
+PARTS = ((0, 256), (256, 256), (512, 128), (640, 128), (768, 128), (896, 128))
 
 FLOPS = 2 * 128 * (1024 + 2048) * 8192
 
@@ -144,12 +141,10 @@ def tile_nascell_w_kernel(
 
         acc = [bank("p47_%d" % c) for c in range(8)]
         order47 = (0, 2, 1, 3, 4, 6, 5, 7)
-        for s0, count, tag in ((0, G_M, "w32k"), (G_M, G_X, "w64k")):
-            wt = load_w(s0, count, 4 * H, 4 * H, tag, 2 if tag == "w32k" else 1)
+        for s in range(G_ALL):
+            wt = load_w(s, 1, 4 * H, 4 * H, "w16k", 6)
             for c in order47:
-                for s in range(s0, s0 + count):
-                    off = 4 * H * (s - s0) + BANK * c
-                    mx_pass(acc[c][:], s, wt, off, 4 * H + BANK * c, BANK, 0, G_ALL - 1)
+                mx_pass(acc[c][:], s, wt, BANK * c, 4 * H + BANK * c, BANK, 0, G_ALL - 1)
         dst47 = (va, vb, vc, vd)
         func47 = (ACT.Tanh, ACT.Sigmoid, ACT.Tanh, ACT.Sigmoid)
         for c in order47:
@@ -168,13 +163,24 @@ def tile_nascell_w_kernel(
 
         nc.sync.dma_start(out=c_sb[:], in_=c_prev)
         acc = [bank("p01_%d" % c) for c in range(4)]
+        acc_m3 = [bank("pm3_%d" % h) for h in range(2)]
+        acc_x3 = [bank("px3_%d" % h) for h in range(2)]
         order01 = (0, 2, 1, 3)
-        for s0, count, tag in ((0, G_M, "w16k"), (G_M, G_X, "w32k")):
-            wt = load_w(s0, count, 0, 2 * H, tag, 2)
+        w_m23 = []
+        for s in range(G_M):
+            wt = load_w(s, 1, 0, 4 * H, "w16k", 6)
+            w_m23.append((wt, 2 * H))
             for c in order01:
-                for s in range(s0, s0 + count):
-                    off = 2 * H * (s - s0) + BANK * c
-                    mx_pass(acc[c][:], s, wt, off, BANK * c, BANK, 0, G_ALL - 1)
+                mx_pass(acc[c][:], s, wt, BANK * c, BANK * c, BANK, 0, G_ALL - 1)
+        for s in range(G_M):
+            for h in range(2):
+                mx_pass(acc_m3[h][:], s, w_m23[s][0], 3 * H + BANK * h, 3 * H + BANK * h, BANK, 0, G_M - 1)
+        for h in range(2):
+            nc.vector.tensor_copy(out=vf[:, half(h)], in_=acc_m3[h][:])
+        for s in range(G_M, G_ALL):
+            wt = load_w(s, 1, 0, 2 * H, "w8k", 4)
+            for c in order01:
+                mx_pass(acc[c][:], s, wt, BANK * c, BANK * c, BANK, 0, G_ALL - 1)
         for h in range(2):
             nc.scalar.activation(out=ve[:, half(h)], in_=acc[h][:], func=ACT.Sigmoid)
         for h in range(2):
@@ -183,65 +189,76 @@ def tile_nascell_w_kernel(
             )
         for h in range(2):
             nc.scalar.activation(out=ve[:, half(h)], in_=ve[:, half(h)], func=ACT.Tanh)
-
-        acc_m3 = [bank("pm3_%d" % h) for h in range(2)]
-        acc_x3 = [bank("px3_%d" % h) for h in range(2)]
-        acc2 = [bank("p2_%d" % i) for i in range(len(PARTS))]
-        wt = load_w(0, G_M, 2 * H, 2 * H, "w16k", 2)
-        for h in range(2):
-            for s in range(G_M):
-                mx_pass(acc_m3[h][:], s, wt, 2 * H * s + H + BANK * h, 3 * H + BANK * h, BANK, 0, G_M - 1)
-        for i, (lo, n) in enumerate(PARTS):
-            for s in range(G_M):
-                mx_pass(acc2[i][:, 0:n], s, wt, 2 * H * s + lo, 2 * H + lo, n, 0, G_ALL - 1)
-        for h in range(2):
-            nc.vector.tensor_copy(out=vf[:, half(h)], in_=acc_m3[h][:])
         for h in range(2):
             nc.vector.tensor_tensor(out=ve[:, half(h)], in0=ve[:, half(h)], in1=c_sb[:, half(h)], op=ALU.add)
         for h in range(2):
             nc.scalar.activation(out=ve[:, half(h)], in_=ve[:, half(h)], func=ACT.Tanh)
         for h in range(2):
             nc.vector.tensor_tensor(out=va[:, half(h)], in0=va[:, half(h)], in1=ve[:, half(h)], op=ALU.mult)
-        wt = load_w(G_M, G_X, 3 * H, H, "w64k", 1)
-        for h in range(2):
+
+        acc2 = [bank("p2_%d" % i) for i in range(len(PARTS))]
+        for i, (lo, n) in enumerate(PARTS):
+            for s in range(G_M):
+                wt, off = w_m23[s]
+                mx_pass(acc2[i][:, 0:n], s, wt, off + lo, 2 * H + lo, n, 0, G_ALL - 1)
+
+        def x3_half(h):
+            wt = load_w(G_M, G_X, 3 * H + BANK * h, BANK, "x3_half", 2)
             for s in range(G_M, G_ALL):
-                off = H * (s - G_M) + BANK * h
-                mx_pass(acc_x3[h][:], s, wt, off, 3 * H + BANK * h, BANK, G_M, G_ALL - 1)
+                mx_pass(acc_x3[h][:], s, wt, BANK * (s - G_M), 3 * H + BANK * h, BANK, G_M, G_ALL - 1)
             nc.vector.tensor_tensor(out=vf[:, half(h)], in0=acc_x3[h][:], in1=vf[:, half(h)], op=ALU.mult)
 
-        z_tiles = []
-        for lo, n, tag, bufs in ((0, BANK, "w32k", 2), (BANK, CH, "w4k", 2), (BANK + CH, CH, "w4k", 2)):
-            wt = load_w(G_M, G_X, 2 * H + lo, n, tag, bufs)
-            for j in range(n // CH):
-                z_tiles.append((wt, lo, n))
+        def load_x2(k, lo, n):
+            return load_w(G_M, G_X, 2 * H + lo, n, "x2_%d" % k, 1), lo, n
 
         def cols(i):
             lo, n = PARTS[i]
             return slice(lo, lo + n)
 
-        for step in range(N_ST + 2):
-            if step < N_ST:
-                wt, w_lo, w_n = z_tiles[step]
-                for i in STEPS[step]:
-                    lo, n = PARTS[i]
-                    for s in range(G_M, G_ALL):
-                        off = w_n * (s - G_M) + lo - w_lo
-                        mx_pass(acc2[i][:, 0:n], s, wt, off, 2 * H + lo, n, 0, G_ALL - 1)
-                    nc.scalar.activation(out=vg[:, cols(i)], in_=acc2[i][:, 0:n], func=ACT.Sigmoid)
-                for i in STEPS[step]:
-                    nc.vector.scalar_tensor_tensor(
-                        out=vg[:, cols(i)], in0=vf[:, cols(i)], scalar=0.0, in1=vg[:, cols(i)], op0=ALU.max, op1=ALU.add
-                    )
-            if 1 <= step <= N_ST:
-                for i in STEPS[step - 1]:
-                    nc.scalar.activation(out=vg[:, cols(i)], in_=vg[:, cols(i)], func=ACT.Tanh)
-                for i in STEPS[step - 1]:
-                    nc.vector.tensor_tensor(out=va[:, cols(i)], in0=va[:, cols(i)], in1=vg[:, cols(i)], op=ALU.mult)
-            if step >= 2:
-                for i in STEPS[step - 2]:
-                    nc.scalar.activation(out=va[:, cols(i)], in_=va[:, cols(i)], func=ACT.Tanh)
-                for i in STEPS[step - 2]:
-                    nc.vector.tensor_tensor(out=ve[:, cols(i)], in0=ve[:, cols(i)], in1=vg[:, cols(i)], op=ALU.mult)
-                whole = slice(CH * (step - 2), CH * (step - 1))
-                nc.sync.dma_start(out=out_1[:, whole], in_=ve[:, whole])
-                nc.sync.dma_start(out=out_0[:, whole], in_=va[:, whole])
+        def step1(parts, z):
+            wt, w_lo, w_n = z
+            for i in parts:
+                lo, n = PARTS[i]
+                for s in range(G_M, G_ALL):
+                    off = w_n * (s - G_M) + lo - w_lo
+                    mx_pass(acc2[i][:, 0:n], s, wt, off, 2 * H + lo, n, 0, G_ALL - 1)
+                nc.scalar.activation(out=vg[:, cols(i)], in_=acc2[i][:, 0:n], func=ACT.Sigmoid)
+            for i in parts:
+                nc.vector.scalar_tensor_tensor(
+                    out=vg[:, cols(i)], in0=vf[:, cols(i)], scalar=0.0, in1=vg[:, cols(i)], op0=ALU.max, op1=ALU.add
+                )
+
+        def step2(parts):
+            for i in parts:
+                nc.scalar.activation(out=vg[:, cols(i)], in_=vg[:, cols(i)], func=ACT.Tanh)
+            for i in parts:
+                nc.vector.tensor_tensor(out=va[:, cols(i)], in0=va[:, cols(i)], in1=vg[:, cols(i)], op=ALU.mult)
+
+        def step3(parts):
+            for i in parts:
+                nc.scalar.activation(out=va[:, cols(i)], in_=va[:, cols(i)], func=ACT.Tanh)
+            for i in parts:
+                nc.vector.tensor_tensor(out=ve[:, cols(i)], in0=ve[:, cols(i)], in1=vg[:, cols(i)], op=ALU.mult)
+
+        def store(lo, n, last=False):
+            pair = ((out_0, va), (out_1, ve))
+            for dst, src in reversed(pair) if last else pair:
+                nc.sync.dma_start(out=dst[:, lo : lo + n], in_=src[:, lo : lo + n])
+
+        x3_half(0)
+        z = load_x2(0, 0, 512)
+        step1((0, 1,), z)
+        step2((0, 1,))
+        step3((0, 1,))
+        x3_half(1)
+        z0 = load_x2(1, 512, 256)
+        z1 = load_x2(2, 768, 256)
+        store(0, 512)
+        step1((2, 3,), z0)
+        step2((2, 3,))
+        step1((4, 5,), z1)
+        step3((2, 3,))
+        store(512, 256, False)
+        step2((4, 5,))
+        step3((4, 5,))
+        store(768, 256, True)

@@ -17,6 +17,7 @@ H = 1024
 G_M = 2
 G_X = 4
 G_ALL = G_M + G_X
+G_J = 2
 BANK = 512
 PARTS = ((0, 256), (256, 256), (512, 128), (640, 128), (768, 128), (896, 128))
 
@@ -141,10 +142,17 @@ def tile_nascell_w_kernel(
 
         acc = [bank("p47_%d" % c) for c in range(8)]
         order47 = (0, 2, 1, 3, 4, 6, 5, 7)
+        w_m23 = []
         for s in range(G_ALL):
-            wt = load_w(s, 1, 4 * H, 4 * H, "w16k", 6)
+            if s < G_J:
+                wt = load_w(s, 1, 0, 8 * H, "w32k", G_J)
+                w_m23.append((wt, 2 * H))
+                off = 4 * H
+            else:
+                wt = load_w(s, 1, 4 * H, 4 * H, "w16k", G_ALL - G_J)
+                off = 0
             for c in order47:
-                mx_pass(acc[c][:], s, wt, BANK * c, 4 * H + BANK * c, BANK, 0, G_ALL - 1)
+                mx_pass(acc[c][:], s, wt, off + BANK * c, 4 * H + BANK * c, BANK, 0, G_ALL - 1)
         dst47 = (va, vb, vc, vd)
         func47 = (ACT.Tanh, ACT.Sigmoid, ACT.Tanh, ACT.Sigmoid)
         for c in order47:
@@ -166,18 +174,18 @@ def tile_nascell_w_kernel(
         acc_m3 = [bank("pm3_%d" % h) for h in range(2)]
         acc_x3 = [bank("px3_%d" % h) for h in range(2)]
         order01 = (0, 2, 1, 3)
-        w_m23 = []
-        for s in range(G_M):
-            wt = load_w(s, 1, 0, 4 * H, "w16k", 6)
-            w_m23.append((wt, 2 * H))
+        for s in range(G_J):
             for c in order01:
-                mx_pass(acc[c][:], s, wt, BANK * c, BANK * c, BANK, 0, G_ALL - 1)
+                mx_pass(acc[c][:], s, w_m23[s][0], BANK * c, BANK * c, BANK, 0, G_ALL - 1)
         for s in range(G_M):
             for h in range(2):
                 mx_pass(acc_m3[h][:], s, w_m23[s][0], 3 * H + BANK * h, 3 * H + BANK * h, BANK, 0, G_M - 1)
         for h in range(2):
             nc.vector.tensor_copy(out=vf[:, half(h)], in_=acc_m3[h][:])
-        for s in range(G_M, G_ALL):
+        for s in range(G_M, G_J):
+            for h in range(2):
+                mx_pass(acc_x3[h][:], s, w_m23[s][0], 3 * H + BANK * h, 3 * H + BANK * h, BANK, G_M, G_ALL - 1)
+        for s in range(G_J, G_ALL):
             wt = load_w(s, 1, 0, 2 * H, "w8k", 4)
             for c in order01:
                 mx_pass(acc[c][:], s, wt, BANK * c, BANK * c, BANK, 0, G_ALL - 1)
@@ -198,18 +206,18 @@ def tile_nascell_w_kernel(
 
         acc2 = [bank("p2_%d" % i) for i in range(len(PARTS))]
         for i, (lo, n) in enumerate(PARTS):
-            for s in range(G_M):
+            for s in range(G_J):
                 wt, off = w_m23[s]
                 mx_pass(acc2[i][:, 0:n], s, wt, off + lo, 2 * H + lo, n, 0, G_ALL - 1)
 
         def x3_half(h):
-            wt = load_w(G_M, G_X, 3 * H + BANK * h, BANK, "x3_half", 2)
-            for s in range(G_M, G_ALL):
-                mx_pass(acc_x3[h][:], s, wt, BANK * (s - G_M), 3 * H + BANK * h, BANK, G_M, G_ALL - 1)
+            wt = load_w(G_J, G_ALL - G_J, 3 * H + BANK * h, BANK, "w16k", G_ALL - G_J)
+            for s in range(G_J, G_ALL):
+                mx_pass(acc_x3[h][:], s, wt, BANK * (s - G_J), 3 * H + BANK * h, BANK, G_M, G_ALL - 1)
             nc.vector.tensor_tensor(out=vf[:, half(h)], in0=acc_x3[h][:], in1=vf[:, half(h)], op=ALU.mult)
 
         def load_x2(k, lo, n):
-            return load_w(G_M, G_X, 2 * H + lo, n, "x2_%d" % k, 1), lo, n
+            return load_w(G_J, G_ALL - G_J, 2 * H + lo, n, "w16k", G_ALL - G_J), lo, n
 
         def cols(i):
             lo, n = PARTS[i]
@@ -219,8 +227,8 @@ def tile_nascell_w_kernel(
             wt, w_lo, w_n = z
             for i in parts:
                 lo, n = PARTS[i]
-                for s in range(G_M, G_ALL):
-                    off = w_n * (s - G_M) + lo - w_lo
+                for s in range(G_J, G_ALL):
+                    off = w_n * (s - G_J) + lo - w_lo
                     mx_pass(acc2[i][:, 0:n], s, wt, off, 2 * H + lo, n, 0, G_ALL - 1)
                 nc.scalar.activation(out=vg[:, cols(i)], in_=acc2[i][:, 0:n], func=ACT.Sigmoid)
             for i in parts:
@@ -228,17 +236,23 @@ def tile_nascell_w_kernel(
                     out=vg[:, cols(i)], in0=vf[:, cols(i)], scalar=0.0, in1=vg[:, cols(i)], op0=ALU.max, op1=ALU.add
                 )
 
-        def step2(parts):
+        def new_c(i):
+            nc.vector.tensor_tensor(out=ve[:, cols(i)], in0=ve[:, cols(i)], in1=vg[:, cols(i)], op=ALU.mult)
+
+        def step2(parts, last=False):
             for i in parts:
                 nc.scalar.activation(out=vg[:, cols(i)], in_=vg[:, cols(i)], func=ACT.Tanh)
             for i in parts:
                 nc.vector.tensor_tensor(out=va[:, cols(i)], in0=va[:, cols(i)], in1=vg[:, cols(i)], op=ALU.mult)
+                if last:
+                    new_c(i)
 
-        def step3(parts):
+        def step3(parts, last=False):
             for i in parts:
                 nc.scalar.activation(out=va[:, cols(i)], in_=va[:, cols(i)], func=ACT.Tanh)
-            for i in parts:
-                nc.vector.tensor_tensor(out=ve[:, cols(i)], in0=ve[:, cols(i)], in1=vg[:, cols(i)], op=ALU.mult)
+            if not last:
+                for i in parts:
+                    new_c(i)
 
         def store(lo, n, last=False):
             pair = ((out_0, va), (out_1, ve))
@@ -259,6 +273,6 @@ def tile_nascell_w_kernel(
         step1((4, 5,), z1)
         step3((2, 3,))
         store(512, 256, False)
-        step2((4, 5,))
-        step3((4, 5,))
+        step2((4, 5,), True)
+        step3((4, 5,), True)
         store(768, 256, True)

from contextlib import ExitStack

import concourse.masks as masks
import concourse.mybir as mybir

F32 = mybir.dt.float32
BF16 = mybir.dt.bfloat16
I32 = mybir.dt.int32
U32 = mybir.dt.uint32
U8 = mybir.dt.uint8
FP8X4 = mybir.dt.float8_e4m3fn_x4
ACT = mybir.ActivationFunctionType
ALU = mybir.AluOpType

P = 128
H = 1024
G_M = 2
G_X = 4
G_ALL = G_M + G_X
G_J = 2
BANK = 512
PARTS = ((0, 256), (256, 256), (512, 128), (640, 128), (768, 128), (896, 128))

FLOPS = 2 * 128 * (1024 + 2048) * 8192


def tile_nascell_w_kernel(
    tc, x, m_prev, c_prev, w_m_words, w_m_scales, w_inputs_words, w_inputs_scales, out_0, out_1
):
    nc = tc.nc
    wm_words = w_m_words.rearrange("g p n t -> g p (n t)").bitcast(I32)
    wi_words = w_inputs_words.rearrange("g p n t -> g p (n t)").bitcast(I32)
    wm_scales = w_m_scales.bitcast(I32)
    wi_scales = w_inputs_scales.bitcast(I32)

    with ExitStack() as ctx:
        const = ctx.enter_context(tc.tile_pool(name="const", bufs=1))
        wpool = ctx.enter_context(tc.tile_pool(name="wring", bufs=6))
        psum = ctx.enter_context(tc.psum_pool(name="psum", bufs=8))
        ctx.enter_context(tc.manual_schedule())

        m_sb = const.tile([P, H], BF16, name="m_sb")
        x_sb = const.tile([P, 2 * H], BF16, name="x_sb")
        c_sb = const.tile([P, H], BF16, name="c_sb")
        nc.sync.dma_start(out=m_sb[:], in_=m_prev)
        nc.sync.dma_start(out=x_sb[:], in_=x)

        planes_m = const.tile([P, G_M * 2048], U8, name="planes_m", align_bytes=64)
        planes_x = const.tile([P, 8 * H], U8, name="planes_x", align_bytes=64)
        nc.vector.memset(planes_x[:].bitcast(I32), 0)
        nc.vector.memset(planes_m[:].bitcast(I32), 0)

        warm = const.tile([P, 16], F32, name="warm")
        nc.vector.memset(warm[:], 0.0)
        nc.scalar.activation(out=warm[:, 8:16], in_=warm[:, 0:8], func=ACT.Sigmoid)

        ident = const.tile([P, P], F32, name="ident")
        masks.make_identity(nc, ident[:])

        for quadrants in ((2, 3), (0, 1)):
            for q in quadrants:
                nc.sync.dma_start(
                    out=planes_x[32 * q : 32 * q + 16, :].bitcast(I32),
                    in_=wi_scales[:, 4 * q : 4 * q + 4, :],
                )
            for q in quadrants:
                for g in range(G_M):
                    nc.sync.dma_start(
                        out=planes_m[32 * q : 32 * q + 16, 2048 * g : 2048 * (g + 1)].bitcast(I32),
                        in_=wm_scales[g, 4 * q : 4 * q + 4, :].rearrange("r (j n) -> j r n", j=4),
                    )

        grouped = const.tile([P, G_ALL * 512], BF16, name="grouped", align_bytes=64)
        grouped_w = grouped[:].bitcast(F32).rearrange("p (s b u) -> p s b u", s=G_ALL, u=2)
        codes = const.tile([P, G_ALL * P], U32, name="codes", align_bytes=64)
        a_scales = const.tile([P, G_ALL * P], U8, name="a_scales", align_bytes=64)

        def transpose_two_groups(src_words, g0, s0, copy):
            tp = psum.tile([P, 2, 2, P], F32, tag="bank", name="tp%d" % s0)
            for g in range(2):
                for u in range(2):
                    lo = 256 * (g0 + g) + u
                    nc.tensor.transpose(tp[:, g, u, :], src_words[:, lo : lo + 255 : 2], ident[:])
            copy(out=grouped_w[:, s0 : s0 + 2], in_=tp[:].rearrange("p g u b -> p g b u"))

        m_words = m_sb[:].bitcast(F32)
        x_words = x_sb[:].bitcast(F32)
        transpose_two_groups(m_words, 0, 0, nc.vector.tensor_copy)
        transpose_two_groups(x_words, 0, 2, nc.scalar.copy)
        transpose_two_groups(x_words, 2, 4, nc.vector.tensor_copy)
        nc.vector.quantize_mx(
            out=codes[:, 0 : G_M * P].bitcast(FP8X4),
            scales=a_scales[:, 0 : G_M * P],
            in_=grouped[:, 0 : G_M * 512],
        )
        nc.vector.quantize_mx(
            out=codes[:, G_M * P :].bitcast(FP8X4),
            scales=a_scales[:, G_M * P :],
            in_=grouped[:, G_M * 512 :],
        )

        def load_w(s, count, n0, n, tag, bufs):
            wt = wpool.tile([P, count * n], U32, tag=tag, bufs=bufs, name="w%d_%d" % (s, n0), align_bytes=64)
            src = wm_words[s : s + count] if s < G_M else wi_words[s - G_M : s - G_M + count]
            nc.sync.dma_start(
                out=wt[:].bitcast(I32).rearrange("p (s n) -> p s n", s=count),
                in_=src[:, :, n0 : n0 + n].rearrange("s p n -> p s n"),
            )
            return wt

        def plane(s, n0, n):
            if s < G_M:
                k = 4 * (n0 // 2048)
                lo = 2048 * s + n0 % 2048
                return planes_m[k:P, lo : lo + n]
            return planes_x[4 * (s - G_M) : P, n0 : n0 + n]

        def mx_pass(acc, s, wt, off, n0, n, first, last):
            nc.tensor.matmul_mx(
                out=acc,
                lhsT=codes[:, P * s : P * (s + 1)].bitcast(FP8X4),
                lhsT_scale=a_scales[:, P * s : P * (s + 1)],
                rhs=wt[:, off : off + n].bitcast(FP8X4),
                rhs_scale=plane(s, n0, n),
                start=(s == first),
                stop=(s == last),
            )

        def bank(name):
            return psum.tile([P, BANK], F32, tag="bank", name=name)

        def half(h):
            return slice(BANK * h, BANK * (h + 1))

        va = const.tile([P, H], F32, name="va")
        vb = const.tile([P, H], F32, name="vb")
        vc = const.tile([P, H], F32, name="vc")
        vd = const.tile([P, H], F32, name="vd")
        ve = const.tile([P, H], F32, name="ve")
        vf = const.tile([P, H], F32, name="vf")
        vg = const.tile([P, H], F32, name="vg")

        acc = [bank("p47_%d" % c) for c in range(8)]
        order47 = (0, 2, 1, 3, 4, 6, 5, 7)
        w_m23 = []
        for s in range(G_ALL):
            if s < G_J:
                wt = load_w(s, 1, 0, 8 * H, "w32k", G_J)
                w_m23.append((wt, 2 * H))
                off = 4 * H
            else:
                wt = load_w(s, 1, 4 * H, 4 * H, "w16k", G_ALL - G_J)
                off = 0
            for c in order47:
                mx_pass(acc[c][:], s, wt, off + BANK * c, 4 * H + BANK * c, BANK, 0, G_ALL - 1)
        dst47 = (va, vb, vc, vd)
        func47 = (ACT.Tanh, ACT.Sigmoid, ACT.Tanh, ACT.Sigmoid)
        for c in order47:
            nc.scalar.activation(out=dst47[c // 2][:, half(c % 2)], in_=acc[c][:], func=func47[c // 2])
        for h in range(2):
            nc.vector.tensor_tensor(out=va[:, half(h)], in0=va[:, half(h)], in1=vb[:, half(h)], op=ALU.mult)
        for h in range(2):
            nc.vector.tensor_tensor(out=vc[:, half(h)], in0=vc[:, half(h)], in1=vd[:, half(h)], op=ALU.add)
        nc.scalar.activation(out=va[:], in_=va[:], func=ACT.Tanh)
        for h in range(2):
            nc.scalar.activation(out=vc[:, half(h)], in_=vc[:, half(h)], func=ACT.Sigmoid)
        for h in range(2):
            nc.vector.tensor_tensor(out=va[:, half(h)], in0=va[:, half(h)], in1=vc[:, half(h)], op=ALU.add)
        for h in range(2):
            nc.scalar.activation(out=va[:, half(h)], in_=va[:, half(h)], func=ACT.Tanh)

        nc.sync.dma_start(out=c_sb[:], in_=c_prev)
        acc = [bank("p01_%d" % c) for c in range(4)]
        acc_m3 = [bank("pm3_%d" % h) for h in range(2)]
        acc_x3 = [bank("px3_%d" % h) for h in range(2)]
        order01 = (0, 2, 1, 3)
        for s in range(G_J):
            for c in order01:
                mx_pass(acc[c][:], s, w_m23[s][0], BANK * c, BANK * c, BANK, 0, G_ALL - 1)
        for s in range(G_M):
            for h in range(2):
                mx_pass(acc_m3[h][:], s, w_m23[s][0], 3 * H + BANK * h, 3 * H + BANK * h, BANK, 0, G_M - 1)
        for h in range(2):
            nc.vector.tensor_copy(out=vf[:, half(h)], in_=acc_m3[h][:])
        for s in range(G_M, G_J):
            for h in range(2):
                mx_pass(acc_x3[h][:], s, w_m23[s][0], 3 * H + BANK * h, 3 * H + BANK * h, BANK, G_M, G_ALL - 1)
        for s in range(G_J, G_ALL):
            wt = load_w(s, 1, 0, 2 * H, "w8k", 4)
            for c in order01:
                mx_pass(acc[c][:], s, wt, BANK * c, BANK * c, BANK, 0, G_ALL - 1)
        for h in range(2):
            nc.scalar.activation(out=ve[:, half(h)], in_=acc[h][:], func=ACT.Sigmoid)
        for h in range(2):
            nc.vector.scalar_tensor_tensor(
                out=ve[:, half(h)], in0=acc[2 + h][:], scalar=0.0, in1=ve[:, half(h)], op0=ALU.max, op1=ALU.mult
            )
        for h in range(2):
            nc.scalar.activation(out=ve[:, half(h)], in_=ve[:, half(h)], func=ACT.Tanh)
        for h in range(2):
            nc.vector.tensor_tensor(out=ve[:, half(h)], in0=ve[:, half(h)], in1=c_sb[:, half(h)], op=ALU.add)
        for h in range(2):
            nc.scalar.activation(out=ve[:, half(h)], in_=ve[:, half(h)], func=ACT.Tanh)
        for h in range(2):
            nc.vector.tensor_tensor(out=va[:, half(h)], in0=va[:, half(h)], in1=ve[:, half(h)], op=ALU.mult)

        acc2 = [bank("p2_%d" % i) for i in range(len(PARTS))]
        for i, (lo, n) in enumerate(PARTS):
            for s in range(G_J):
                wt, off = w_m23[s]
                mx_pass(acc2[i][:, 0:n], s, wt, off + lo, 2 * H + lo, n, 0, G_ALL - 1)

        def x3_half(h):
            wt = load_w(G_J, G_ALL - G_J, 3 * H + BANK * h, BANK, "w16k", G_ALL - G_J)
            for s in range(G_J, G_ALL):
                mx_pass(acc_x3[h][:], s, wt, BANK * (s - G_J), 3 * H + BANK * h, BANK, G_M, G_ALL - 1)
            nc.vector.tensor_tensor(out=vf[:, half(h)], in0=acc_x3[h][:], in1=vf[:, half(h)], op=ALU.mult)

        def load_x2(k, lo, n):
            return load_w(G_J, G_ALL - G_J, 2 * H + lo, n, "w16k", G_ALL - G_J), lo, n

        def cols(i):
            lo, n = PARTS[i]
            return slice(lo, lo + n)

        def step1(parts, z):
            wt, w_lo, w_n = z
            for i in parts:
                lo, n = PARTS[i]
                for s in range(G_J, G_ALL):
                    off = w_n * (s - G_J) + lo - w_lo
                    mx_pass(acc2[i][:, 0:n], s, wt, off, 2 * H + lo, n, 0, G_ALL - 1)
                nc.scalar.activation(out=vg[:, cols(i)], in_=acc2[i][:, 0:n], func=ACT.Sigmoid)
            for i in parts:
                nc.vector.scalar_tensor_tensor(
                    out=vg[:, cols(i)], in0=vf[:, cols(i)], scalar=0.0, in1=vg[:, cols(i)], op0=ALU.max, op1=ALU.add
                )

        def new_c(i):
            nc.vector.tensor_tensor(out=ve[:, cols(i)], in0=ve[:, cols(i)], in1=vg[:, cols(i)], op=ALU.mult)

        def step2(parts, last=False):
            for i in parts:
                nc.scalar.activation(out=vg[:, cols(i)], in_=vg[:, cols(i)], func=ACT.Tanh)
            for i in parts:
                nc.vector.tensor_tensor(out=va[:, cols(i)], in0=va[:, cols(i)], in1=vg[:, cols(i)], op=ALU.mult)
                if last:
                    new_c(i)

        def step3(parts, last=False):
            for i in parts:
                nc.scalar.activation(out=va[:, cols(i)], in_=va[:, cols(i)], func=ACT.Tanh)
            if not last:
                for i in parts:
                    new_c(i)

        def store(lo, n, last=False):
            pair = ((out_0, va), (out_1, ve))
            for dst, src in reversed(pair) if last else pair:
                nc.sync.dma_start(out=dst[:, lo : lo + n], in_=src[:, lo : lo + n])

        x3_half(0)
        z = load_x2(0, 0, 512)
        step1((0, 1,), z)
        step2((0, 1,))
        step3((0, 1,))
        x3_half(1)
        z0 = load_x2(1, 512, 256)
        z1 = load_x2(2, 768, 256)
        store(0, 512)
        step1((2, 3,), z0)
        step2((2, 3,))
        step1((4, 5,), z1)
        step3((2, 3,))
        store(512, 256, False)
        step2((4, 5,), True)
        step3((4, 5,), True)
        store(768, 256, True)
